import numpy as np
import ml_dtypes


BF16 = ml_dtypes.bfloat16


def bf(x):
    return np.asarray(x, np.float32).astype(BF16)


def f64(x):
    return np.asarray(x).astype(np.float64)


E2M1 = np.array([0.0, 0.5, 1.0, 1.5, 2.0, 3.0, 4.0, 6.0, -0.0, -0.5, -1.0, -1.5, -2.0, -3.0, -4.0, -6.0])


def pack_weight(w, fmt):
    k, n = w.shape
    w = f64(bf(w)).reshape(k // 32, 32, n)
    amax = np.abs(w).max(1)
    if fmt == "e4m3":
        byte = np.frexp(amax)[1] - 1 + 127 - 7
    else:
        mant, ex = np.frexp(amax / 6.0)
        byte = np.where(mant > 0.5, ex, ex - 1) + 127
    byte = np.clip(np.where(amax > 0, byte, 1), 1, 254)
    scaled = (w * np.exp2(127.0 - byte)[:, None, :]).reshape(k, n).astype(np.float32)
    by_word = np.ascontiguousarray(scaled.reshape(k // 512, 128, 4, n).transpose(0, 1, 3, 2))
    if fmt == "e4m3":
        words = by_word.astype(ml_dtypes.float8_e4m3fn).view(np.uint8)
    else:
        c = by_word.astype(ml_dtypes.float4_e2m1fn).view(np.uint8) & 0xF
        words = c[..., 0::2] | (c[..., 1::2] << 4)
    return np.ascontiguousarray(words), np.ascontiguousarray(byte.astype(np.uint8).reshape(k // 512, 16, n))


def unpack_weight(words, scales, fmt):
    g, p, n, _ = words.shape
    if fmt == "e4m3":
        vals = np.ascontiguousarray(words).view(ml_dtypes.float8_e4m3fn).astype(np.float64)
    else:
        nib = np.empty((g, p, n, 4), np.uint8)
        nib[..., 0::2] = words & 0xF
        nib[..., 1::2] = words >> 4
        vals = E2M1[nib]
    vals = vals * np.repeat(np.exp2(scales.astype(np.float64) - 127.0), 8, axis=1)[..., None]
    return vals.transpose(0, 1, 3, 2).reshape(g * 512, n)

def pack4(w):
    words, scales = pack_weight(w, "e2m1")
    return words.reshape(words.shape[0], 128, -1), scales


def unpack4(words, scales):
    return unpack_weight(words.reshape(words.shape[0], 128, -1, 2), scales, "e2m1")


def kspread(k):
    return np.exp2(np.repeat(np.random.randint(-6, 7, k // 32), 32).astype(np.float64))


B, T, E, C, H, XB = 1, 512, 1536, 1536, 16, 512
SCALE_BASE = float(XB)


def rotate_every_two(z):
    z1 = z[..., ::2]
    z2 = z[..., 1::2]
    return np.stack([-z2, z1], axis=-1).reshape(z.shape)


def xpos(z):
    dim_scale = (f64(np.arange(0, C, 2)) + 0.4 * C) / (1.4 * C)
    pos = f64(np.arange(T))
    scale = dim_scale[None, :] ** (pos[:, None] / SCALE_BASE)
    inv_freq = 1.0 / (10000.0 ** (f64(np.arange(0, C, 2)) / C))
    sinusoid = pos[:, None] * inv_freq[None, :]
    sin = np.repeat(np.sin(sinusoid) * scale, 2, axis=-1)
    cos = np.repeat(np.cos(sinusoid) * scale, 2, axis=-1)
    return z * cos[None] + rotate_every_two(z) * sin[None]


def setup_inputs():
    s = kspread(E)
    x = np.random.standard_normal((B, T, E)) * s
    x_words, x_scales = pack4(x.reshape(B * T, E).T)
    w_q_words, w_q_scales = pack4(np.random.standard_normal((E, C)) * 0.5 / np.sqrt(E) / s[:, None])
    w_k_words, w_k_scales = pack4(np.random.standard_normal((E, C)) * 0.5 / np.sqrt(E) / s[:, None])
    return {"x_words": x_words, "x_scales": x_scales,
            "w_q_words": w_q_words, "w_q_scales": w_q_scales,
            "w_k_words": w_k_words, "w_k_scales": w_k_scales}


def reference(x_words, x_scales, w_q_words, w_q_scales, w_k_words, w_k_scales):
    xq = unpack4(x_words, x_scales).T.reshape(B, T, E)
    q = xq @ unpack4(w_q_words, w_q_scales)
    k = xq @ unpack4(w_k_words, w_k_scales)
    return xpos(q), xpos(k)

@@ -1,0 +1,219 @@
+import math
+from contextlib import ExitStack
+
+import concourse.mybir as mybir
+
+F32 = mybir.dt.float32
+I32 = mybir.dt.int32
+U8 = mybir.dt.uint8
+FP4X4 = mybir.dt.float4_e2m1fn_x4
+ALU = mybir.AluOpType
+ACT = mybir.ActivationFunctionType
+
+P = 128
+T = 512
+E = 1536
+C = 1536
+PASSES = E // 512
+TILES = T // P
+PAIRS = C // 2
+BANK = 512
+BANK_PAIRS = BANK // 2
+CHUNKS = C // BANK
+SCALE_BASE = 512.0
+
+FLOPS = 2 * 2 * T * E * C
+
+DIRECT = (312, 368, 408, 432)
+LOW = DIRECT[-1]
+HEAD = 2 * BANK_PAIRS
+
+
+def tile_multiscaleretention_pa_kernel(
+    tc, x_words, x_scales, w_q_words, w_q_scales, w_k_words, w_k_scales, out_0, out_1
+):
+    nc = tc.nc
+    words = (w_q_words, w_k_words)
+    scales = (w_q_scales, w_k_scales)
+    outs = (out_0, out_1)
+
+    with ExitStack() as ctx:
+        keep = ctx.enter_context(tc.tile_pool(name="keep", bufs=1))
+        tabs = ctx.enter_context(tc.tile_pool(name="tabs", bufs=TILES))
+        work = ctx.enter_context(tc.tile_pool(name="work", bufs=6))
+        psum = ctx.enter_context(tc.psum_pool(name="psum", bufs=8))
+        ctx.enter_context(tc.manual_schedule())
+
+        def plane_tile(cols, name):
+            t = keep.tile([P, PASSES, cols], U8, name=name, align_bytes=64)
+            return t
+
+        def zero(plane):
+            nc.vector.memset(plane[:].rearrange("p g n -> p (g n)").bitcast(I32), 0)
+
+        def load_codes(tile, src, c0, cols):
+            nc.sync.dma_start(
+                out=tile[:].bitcast(I32),
+                in_=src[:, :, 2 * c0 : 2 * (c0 + cols)].rearrange("g p b -> p g b").bitcast(I32),
+            )
+
+        def load_scales(plane, src, c0, cols):
+            for quad in range(4):
+                nc.sync.dma_start(
+                    out=plane[32 * quad : 32 * quad + 4, :, :].bitcast(I32),
+                    in_=src[:, 4 * quad : 4 * quad + 4, c0 : c0 + cols].rearrange("g r n -> r g n").bitcast(I32),
+                )
+
+        x_codes = keep.tile([P, PASSES, 2 * T], U8, name="x_codes", align_bytes=64)
+        x_plane = plane_tile(T, "x_plane")
+        w_codes = {}
+        w_plane = {}
+        for w in range(2):
+            for ch in range(CHUNKS):
+                w_codes[w, ch] = keep.tile([P, PASSES, 2 * BANK], U8, name=f"w_codes_{w}_{ch}", align_bytes=64)
+            w_plane[w, 2] = plane_tile(BANK, f"w_plane_hi_{w}")
+            w_plane[w, 0] = plane_tile(2 * BANK, f"w_plane_lo_{w}")
+
+        for plane in (x_plane, w_plane[0, 2], w_plane[1, 2]):
+            zero(plane)
+
+        arg = keep.tile([P, PAIRS], F32, name="arg")
+        nc.gpsimd.iota(arg[:], pattern=[[10, PAIRS]], base=3072, channel_multiplier=0, allow_small_or_imprecise_dtypes=True)
+        pos = keep.tile([P, TILES], F32, name="pos")
+        nc.gpsimd.iota(pos[:], pattern=[[P, TILES]], base=0, channel_multiplier=1, allow_small_or_imprecise_dtypes=True)
+        pos_r = keep.tile([P, TILES], F32, name="pos_r")
+        nc.gpsimd.tensor_scalar(out=pos_r[:], in0=pos[:], scalar1=1.0 / SCALE_BASE, scalar2=0.0, op0=ALU.mult, op1=ALU.add)
+        pos_a = keep.tile([P, TILES], F32, name="pos_a")
+        nc.gpsimd.tensor_scalar(out=pos_a[:], in0=pos[:], scalar1=2.0 * math.pi, scalar2=0.0, op0=ALU.mult, op1=ALU.add)
+        neg_a = keep.tile([P, TILES], F32, name="neg_a")
+        nc.gpsimd.tensor_scalar(out=neg_a[:], in0=pos[:], scalar1=-2.0 * math.pi, scalar2=0.0, op0=ALU.mult, op1=ALU.add)
+
+        freq = keep.tile([P, PAIRS], F32, name="freq")
+        nc.vector.memset(freq[:, 0:1], 1.0)
+        nc.vector.tensor_scalar(out=freq[:, 0:1], in0=freq[:, 0:1], scalar1=0.5 / math.pi, scalar2=None, op0=ALU.mult)
+        have = 1
+        while have < PAIRS:
+            n = min(have, PAIRS - have)
+            nc.vector.tensor_scalar(
+                out=freq[:, have : have + n], in0=freq[:, 0:n], scalar1=10000.0 ** (-have / PAIRS), scalar2=None, op0=ALU.mult
+            )
+            have += n
+
+        zero(w_plane[0, 0])
+        zero(w_plane[1, 0])
+
+        load_codes(x_codes, x_words, 0, T)
+        load_codes(w_codes[0, 2], words[0], 2 * BANK, BANK)
+        load_scales(x_plane, x_scales, 0, T)
+        load_scales(w_plane[0, 2], scales[0], 2 * BANK, BANK)
+        load_codes(w_codes[1, 2], words[1], 2 * BANK, BANK)
+        load_scales(w_plane[1, 2], scales[1], 2 * BANK, BANK)
+        for w in range(2):
+            load_codes(w_codes[w, 1], words[w], BANK, BANK)
+            load_scales(w_plane[w, 0], scales[w], 0, 2 * BANK)
+        for w in range(2):
+            load_codes(w_codes[w, 0], words[w], 0, BANK)
+
+        frac = {}
+        decay = {}
+        sin = {}
+        cos = {}
+        c_tab = {}
+        s_tab = {}
+
+        def reduce_angle(i):
+            lim = DIRECT[i]
+            turns = tabs.tile([P, LOW], I32, name="turns")
+            nc.vector.tensor_scalar(out=turns[:, :lim], in0=freq[:, :lim], scalar1=pos[:, i : i + 1], scalar2=None, op0=ALU.mult)
+            f = tabs.tile([P, LOW], F32, name="frac")
+            nc.vector.scalar_tensor_tensor(
+                out=f[:, :lim], in0=freq[:, :lim], scalar=pos[:, i : i + 1], in1=turns[:, :lim], op0=ALU.mult, op1=ALU.subtract
+            )
+            frac[i] = f
+
+        def make_decay(i):
+            decay[i] = tabs.tile([P, PAIRS], F32, name="decay")
+            nc.scalar.activation(out=decay[i][:], in_=arg[:], func=ACT.Exp, scale=pos_r[:, i : i + 1])
+
+        def make_sin_cos(i, a, b):
+            lim = DIRECT[i]
+            if i not in sin:
+                sin[i] = tabs.tile([P, PAIRS], F32, name="sin")
+                cos[i] = tabs.tile([P, PAIRS], F32, name="cos")
+            lo = max(a, lim)
+            nc.scalar.activation(out=cos[i][:, lo:b], in_=freq[:, lo:b], func=ACT.Sin, scale=neg_a[:, i : i + 1], bias=half_pi[:, 0:1])
+            nc.scalar.activation(out=sin[i][:, lo:b], in_=freq[:, lo:b], func=ACT.Sin, scale=pos_a[:, i : i + 1])
+            if a < lim:
+                mag = tabs.tile([P, LOW], F32, name="mag")
+                nc.scalar.activation(out=mag[:, a:lim], in_=frac[i][:, a:lim], func=ACT.Abs)
+                nc.scalar.activation(out=cos[i][:, a:lim], in_=mag[:, a:lim], func=ACT.Sin, scale=-2.0 * math.pi, bias=half_pi[:, 0:1])
+                nc.scalar.activation(out=sin[i][:, a:lim], in_=frac[i][:, a:lim], func=ACT.Sin, scale=2.0 * math.pi)
+
+        def make_tables(i, a, b):
+            if i not in c_tab:
+                c_tab[i] = tabs.tile([P, PAIRS], F32, name="c_tab")
+                s_tab[i] = tabs.tile([P, PAIRS], F32, name="s_tab")
+            nc.vector.tensor_tensor(out=c_tab[i][:, a:b], in0=cos[i][:, a:b], in1=decay[i][:, a:b], op=ALU.mult)
+            nc.vector.tensor_tensor(out=s_tab[i][:, a:b], in0=sin[i][:, a:b], in1=decay[i][:, a:b], op=ALU.mult)
+
+        half_pi = keep.tile([P, 1], F32, name="half_pi")
+        nc.gpsimd.tensor_scalar(out=half_pi[:], in0=pos[:, 0:1], scalar1=0.0, scalar2=0.5 * math.pi, op0=ALU.mult, op1=ALU.add)
+
+        nc.scalar.activation(out=arg[:], in_=arg[:], func=ACT.Ln, scale=1.0 / 10752.0)
+        make_decay(0)
+        make_decay(1)
+        reduce_angle(0)
+        for i in range(1, TILES):
+            reduce_angle(i)
+        make_sin_cos(0, HEAD, PAIRS)
+        make_sin_cos(0, 0, HEAD)
+        make_sin_cos(1, 0, PAIRS)
+        make_decay(2)
+        make_decay(3)
+        make_sin_cos(2, 0, PAIRS)
+        make_sin_cos(3, 0, PAIRS)
+
+        def project(i, w, ch):
+            z = psum.tile([P, BANK], F32, name="z")
+            tok = slice(P * i, P * (i + 1))
+            plane = w_plane[w, 2] if ch == 2 else w_plane[w, 0]
+            c0 = 0 if ch == 2 else BANK * ch
+            for g in range(PASSES):
+                nc.tensor.matmul_mx(
+                    out=z[:],
+                    lhsT=x_codes[:, g, 2 * P * i : 2 * P * (i + 1)].bitcast(FP4X4),
+                    lhsT_scale=x_plane[:, g, tok],
+                    rhs=w_codes[w, ch][:, g, :].bitcast(FP4X4),
+                    rhs_scale=plane[:, g, c0 : c0 + BANK],
+                    start=(g == 0),
+                    stop=(g == PASSES - 1),
+                )
+            return z
+
+        def rotate(i, w, ch, z, last):
+            j = slice(BANK_PAIRS * ch, BANK_PAIRS * (ch + 1))
+            zp = z[:].rearrange("p (j t) -> p j t", t=2)
+            a = work.tile([P, BANK], F32, name="a")
+            ap = a[:].rearrange("p (j t) -> p j t", t=2)
+            nc.vector.tensor_tensor(
+                out=ap, in0=zp, in1=c_tab[i][:, j].unsqueeze(2).to_broadcast([P, BANK_PAIRS, 2]), op=ALU.mult
+            )
+            b = work.tile([P, 2, BANK_PAIRS], F32, name="b")
+            nc.vector.scalar_tensor_tensor(out=b[:, 0, :], in0=zp[:, :, 1], scalar=-1.0, in1=s_tab[i][:, j], op0=ALU.mult, op1=ALU.mult)
+            nc.vector.tensor_tensor(out=b[:, 1, :], in0=zp[:, :, 0], in1=s_tab[i][:, j], op=ALU.mult)
+            y = work.tile([P, BANK], F32, name="y")
+            yp = y[:].rearrange("p (j t) -> p j t", t=2)
+            engine = nc.vector if last else nc.gpsimd
+            engine.tensor_tensor(out=yp, in0=ap, in1=b[:].rearrange("p t j -> p j t"), op=ALU.add)
+            nc.sync.dma_start(out=outs[w][0, P * i : P * (i + 1), BANK * ch : BANK * (ch + 1)], in_=y[:])
+
+        make_tables(0, HEAD, PAIRS)
+        for i in range(TILES):
+            for ch in (2, 1, 0):
+                for w in range(2):
+                    z = project(i, w, ch)
+                    rotate(i, w, ch, z, i == TILES - 1 and ch == 0 and w == 1)
+                if i == 0 and ch == 2:
+                    make_tables(0, 0, HEAD)
+                if i + 1 < TILES and ch == 1:
+                    make_tables(i + 1, 0, PAIRS)

@@ -2,6 +2,7 @@ import math
 from contextlib import ExitStack
 
 import concourse.mybir as mybir
+from concourse.masks import make_identity
 
 F32 = mybir.dt.float32
 I32 = mybir.dt.int32
@@ -27,6 +28,9 @@ FLOPS = 2 * 2 * T * E * C
 DIRECT = (312, 368, 408, 432)
 LOW = DIRECT[-1]
 HEAD = 2 * BANK_PAIRS
+LEAD = 4
+ADDS = "GGGPGGPGGGGVPGGGGGGPPGVV"
+INTERLEAVE_FROM = 6
 
 
 def tile_multiscaleretention_pa_kernel(
@@ -40,16 +44,17 @@ def tile_multiscaleretention_pa_kernel(
     with ExitStack() as ctx:
         keep = ctx.enter_context(tc.tile_pool(name="keep", bufs=1))
         tabs = ctx.enter_context(tc.tile_pool(name="tabs", bufs=TILES))
-        work = ctx.enter_context(tc.tile_pool(name="work", bufs=6))
-        psum = ctx.enter_context(tc.psum_pool(name="psum", bufs=8))
+        work = ctx.enter_context(tc.tile_pool(name="work", bufs=10))
+        psum = ctx.enter_context(tc.psum_pool(name="psum", bufs=6))
+        psum_y = ctx.enter_context(tc.psum_pool(name="psum_y", bufs=2))
         ctx.enter_context(tc.manual_schedule())
 
         def plane_tile(cols, name):
             t = keep.tile([P, PASSES, cols], U8, name=name, align_bytes=64)
             return t
 
-        def zero(plane):
-            nc.vector.memset(plane[:].rearrange("p g n -> p (g n)").bitcast(I32), 0)
+        def zero(engine, plane):
+            engine.memset(plane[:].rearrange("p g n -> p (g n)").bitcast(I32), 0)
 
         def load_codes(tile, src, c0, cols):
             nc.sync.dma_start(
@@ -74,8 +79,8 @@ def tile_multiscaleretention_pa_kernel(
             w_plane[w, 2] = plane_tile(BANK, f"w_plane_hi_{w}")
             w_plane[w, 0] = plane_tile(2 * BANK, f"w_plane_lo_{w}")
 
-        for plane in (x_plane, w_plane[0, 2], w_plane[1, 2]):
-            zero(plane)
+        zero(nc.vector, x_plane)
+        zero(nc.vector, w_plane[0, 2])
 
         arg = keep.tile([P, PAIRS], F32, name="arg")
         nc.gpsimd.iota(arg[:], pattern=[[10, PAIRS]], base=3072, channel_multiplier=0, allow_small_or_imprecise_dtypes=True)
@@ -88,6 +93,14 @@ def tile_multiscaleretention_pa_kernel(
         neg_a = keep.tile([P, TILES], F32, name="neg_a")
         nc.gpsimd.tensor_scalar(out=neg_a[:], in0=pos[:], scalar1=-2.0 * math.pi, scalar2=0.0, op0=ALU.mult, op1=ALU.add)
 
+        half_pi = keep.tile([P, 1], F32, name="half_pi")
+        nc.gpsimd.tensor_scalar(out=half_pi[:], in0=pos[:, 0:1], scalar1=0.0, scalar2=0.5 * math.pi, op0=ALU.mult, op1=ALU.add)
+        zero(nc.gpsimd, w_plane[1, 2])
+        zero(nc.gpsimd, w_plane[0, 0])
+        zero(nc.gpsimd, w_plane[1, 0])
+        ident = keep.tile([P, P], F32, name="ident")
+        make_identity(nc, ident[:])
+
         freq = keep.tile([P, PAIRS], F32, name="freq")
         nc.vector.memset(freq[:, 0:1], 1.0)
         nc.vector.tensor_scalar(out=freq[:, 0:1], in0=freq[:, 0:1], scalar1=0.5 / math.pi, scalar2=None, op0=ALU.mult)
@@ -98,9 +111,6 @@ def tile_multiscaleretention_pa_kernel(
                 out=freq[:, have : have + n], in0=freq[:, 0:n], scalar1=10000.0 ** (-have / PAIRS), scalar2=None, op0=ALU.mult
             )
             have += n
-
-        zero(w_plane[0, 0])
-        zero(w_plane[1, 0])
 
         load_codes(x_codes, x_words, 0, T)
         load_codes(w_codes[0, 2], words[0], 2 * BANK, BANK)
@@ -142,22 +152,23 @@ def tile_multiscaleretention_pa_kernel(
                 cos[i] = tabs.tile([P, PAIRS], F32, name="cos")
             lo = max(a, lim)
             nc.scalar.activation(out=cos[i][:, lo:b], in_=freq[:, lo:b], func=ACT.Sin, scale=neg_a[:, i : i + 1], bias=half_pi[:, 0:1])
-            nc.scalar.activation(out=sin[i][:, lo:b], in_=freq[:, lo:b], func=ACT.Sin, scale=pos_a[:, i : i + 1])
             if a < lim:
                 mag = tabs.tile([P, LOW], F32, name="mag")
                 nc.scalar.activation(out=mag[:, a:lim], in_=frac[i][:, a:lim], func=ACT.Abs)
                 nc.scalar.activation(out=cos[i][:, a:lim], in_=mag[:, a:lim], func=ACT.Sin, scale=-2.0 * math.pi, bias=half_pi[:, 0:1])
+            nc.scalar.activation(out=sin[i][:, lo:b], in_=freq[:, lo:b], func=ACT.Sin, scale=pos_a[:, i : i + 1])
+            if a < lim:
                 nc.scalar.activation(out=sin[i][:, a:lim], in_=frac[i][:, a:lim], func=ACT.Sin, scale=2.0 * math.pi)
 
-        def make_tables(i, a, b):
+        def make_c(engine, i, a=0, b=PAIRS):
             if i not in c_tab:
                 c_tab[i] = tabs.tile([P, PAIRS], F32, name="c_tab")
-                s_tab[i] = tabs.tile([P, PAIRS], F32, name="s_tab")
-            nc.vector.tensor_tensor(out=c_tab[i][:, a:b], in0=cos[i][:, a:b], in1=decay[i][:, a:b], op=ALU.mult)
-            nc.vector.tensor_tensor(out=s_tab[i][:, a:b], in0=sin[i][:, a:b], in1=decay[i][:, a:b], op=ALU.mult)
+            engine.tensor_tensor(out=c_tab[i][:, a:b], in0=cos[i][:, a:b], in1=decay[i][:, a:b], op=ALU.mult)
 
-        half_pi = keep.tile([P, 1], F32, name="half_pi")
-        nc.gpsimd.tensor_scalar(out=half_pi[:], in0=pos[:, 0:1], scalar1=0.0, scalar2=0.5 * math.pi, op0=ALU.mult, op1=ALU.add)
+        def make_s(engine, i, a=0, b=PAIRS):
+            if i not in s_tab:
+                s_tab[i] = tabs.tile([P, PAIRS], F32, name="s_tab")
+            engine.tensor_tensor(out=s_tab[i][:, a:b], in0=sin[i][:, a:b], in1=decay[i][:, a:b], op=ALU.mult)
 
         nc.scalar.activation(out=arg[:], in_=arg[:], func=ACT.Ln, scale=1.0 / 10752.0)
         make_decay(0)
@@ -168,10 +179,6 @@ def tile_multiscaleretention_pa_kernel(
         make_sin_cos(0, HEAD, PAIRS)
         make_sin_cos(0, 0, HEAD)
         make_sin_cos(1, 0, PAIRS)
-        make_decay(2)
-        make_decay(3)
-        make_sin_cos(2, 0, PAIRS)
-        make_sin_cos(3, 0, PAIRS)
 
         def project(i, w, ch):
             z = psum.tile([P, BANK], F32, name="z")
@@ -190,30 +197,100 @@ def tile_multiscaleretention_pa_kernel(
                 )
             return z
 
-        def rotate(i, w, ch, z, last):
+        def times_cos(i, ch, z):
             j = slice(BANK_PAIRS * ch, BANK_PAIRS * (ch + 1))
-            zp = z[:].rearrange("p (j t) -> p j t", t=2)
             a = work.tile([P, BANK], F32, name="a")
-            ap = a[:].rearrange("p (j t) -> p j t", t=2)
             nc.vector.tensor_tensor(
-                out=ap, in0=zp, in1=c_tab[i][:, j].unsqueeze(2).to_broadcast([P, BANK_PAIRS, 2]), op=ALU.mult
+                out=a[:].rearrange("p (t j) -> p t j", t=2),
+                in0=z[:].rearrange("p (j t) -> p t j", t=2),
+                in1=c_tab[i][:, j].unsqueeze(1).to_broadcast([P, 2, BANK_PAIRS]),
+                op=ALU.mult,
             )
-            b = work.tile([P, 2, BANK_PAIRS], F32, name="b")
-            nc.vector.scalar_tensor_tensor(out=b[:, 0, :], in0=zp[:, :, 1], scalar=-1.0, in1=s_tab[i][:, j], op0=ALU.mult, op1=ALU.mult)
-            nc.vector.tensor_tensor(out=b[:, 1, :], in0=zp[:, :, 0], in1=s_tab[i][:, j], op=ALU.mult)
-            y = work.tile([P, BANK], F32, name="y")
-            yp = y[:].rearrange("p (j t) -> p j t", t=2)
-            engine = nc.vector if last else nc.gpsimd
-            engine.tensor_tensor(out=yp, in0=ap, in1=b[:].rearrange("p t j -> p j t"), op=ALU.add)
+            return a
+
+        def times_sin(i, ch, z):
+            j = slice(BANK_PAIRS * ch, BANK_PAIRS * (ch + 1))
+            z_pairs = z[:].rearrange("p (j t) -> p j t", t=2)
+            b = work.tile([P, BANK], F32, name="b")
+            nc.vector.scalar_tensor_tensor(
+                out=b[:, :BANK_PAIRS], in0=z_pairs[:, :, 1], scalar=-1.0, in1=s_tab[i][:, j], op0=ALU.mult, op1=ALU.mult
+            )
+            nc.vector.tensor_tensor(out=b[:, BANK_PAIRS:], in0=z_pairs[:, :, 0], in1=s_tab[i][:, j], op=ALU.mult)
+            return b
+
+        def store(n, y):
+            i, w, ch = banks[n]
             nc.sync.dma_start(out=outs[w][0, P * i : P * (i + 1), BANK * ch : BANK * (ch + 1)], in_=y[:])
 
-        make_tables(0, HEAD, PAIRS)
-        for i in range(TILES):
-            for ch in (2, 1, 0):
-                for w in range(2):
-                    z = project(i, w, ch)
-                    rotate(i, w, ch, z, i == TILES - 1 and ch == 0 and w == 1)
-                if i == 0 and ch == 2:
-                    make_tables(0, 0, HEAD)
-                if i + 1 < TILES and ch == 1:
-                    make_tables(i + 1, 0, PAIRS)
+        def add_on_vector(n, a, b):
+            y = work.tile([P, BANK], F32, name="y")
+            nc.vector.tensor_tensor(
+                out=y[:].rearrange("p (j t) -> p j t", t=2),
+                in0=a[:].rearrange("p (t j) -> p j t", t=2),
+                in1=b[:].rearrange("p (t j) -> p j t", t=2),
+                op=ALU.add,
+            )
+            store(n, y)
+
+        def interleave(n, d):
+            y = work.tile([P, BANK], F32, name="y")
+            nc.scalar.copy(
+                out=y[:].rearrange("p (j t) -> p j t", t=2), in_=d[:].rearrange("p (t j) -> p j t", t=2)
+            )
+            store(n, y)
+
+        def add_halves(n, a, b):
+            if ADDS[n] == "P":
+                d = psum_y.tile([P, BANK], F32, name="d_psum")
+                nc.tensor.matmul(out=d[:], lhsT=ident[:], rhs=a[:], start=True, stop=False)
+                nc.tensor.matmul(out=d[:], lhsT=ident[:], rhs=b[:], start=False, stop=True)
+            else:
+                d = work.tile([P, BANK], F32, name="d")
+                nc.gpsimd.tensor_tensor(out=d[:], in0=a[:], in1=b[:], op=ALU.add)
+            return d
+
+        banks = [(i, w, ch) for i in range(TILES) for ch in (2, 1, 0) for w in range(2)]
+        z = {}
+        for n in range(LEAD):
+            z[n] = project(*banks[n])
+        make_c(nc.vector, 0, HEAD, PAIRS)
+        halves = []
+        on_vector = []
+        for n, (i, w, ch) in enumerate(banks):
+            if n + LEAD < len(banks):
+                z[n + LEAD] = project(*banks[n + LEAD])
+            a = times_cos(i, ch, z[n])
+            if n == 0:
+                make_s(nc.vector, 0, HEAD, PAIRS)
+            for args in on_vector:
+                add_on_vector(*args)
+            on_vector = []
+            b = times_sin(i, ch, z[n])
+            if ADDS[n] == "V":
+                on_vector.append((n, a, b))
+            else:
+                halves.append((n, add_halves(n, a, b)))
+            if n >= INTERLEAVE_FROM:
+                for args in halves:
+                    interleave(*args)
+                halves = []
+            if n == 0:
+                make_decay(2)
+            elif n == 1:
+                make_c(nc.vector, 0, 0, HEAD)
+                make_s(nc.vector, 0, 0, HEAD)
+                make_c(nc.gpsimd, 1)
+                make_s(nc.vector, 1)
+                make_decay(3)
+            elif n == 4:
+                make_sin_cos(2, 0, PAIRS)
+                make_s(nc.gpsimd, 2)
+                make_c(nc.gpsimd, 2)
+            elif n == 5:
+                make_sin_cos(3, 0, PAIRS)
+            elif n == 10:
+                make_s(nc.gpsimd, 3)
+            elif n == 12:
+                make_c(nc.gpsimd, 3)
+        for args in on_vector:
+            add_on_vector(*args)

@@ -28,9 +28,8 @@ FLOPS = 2 * 2 * T * E * C
 DIRECT = (312, 368, 408, 432)
 LOW = DIRECT[-1]
 HEAD = 2 * BANK_PAIRS
-LEAD = 4
-ADDS = "GGGPGGPGGGGVPGGGGGGPPGVV"
-INTERLEAVE_FROM = 6
+LEAD = 2
+ADDS = "GPGGPGGGGPGV"
 
 
 def tile_multiscaleretention_pa_kernel(
@@ -44,7 +43,7 @@ def tile_multiscaleretention_pa_kernel(
     with ExitStack() as ctx:
         keep = ctx.enter_context(tc.tile_pool(name="keep", bufs=1))
         tabs = ctx.enter_context(tc.tile_pool(name="tabs", bufs=TILES))
-        work = ctx.enter_context(tc.tile_pool(name="work", bufs=10))
+        work = ctx.enter_context(tc.tile_pool(name="work", bufs=5))
         psum = ctx.enter_context(tc.psum_pool(name="psum", bufs=6))
         psum_y = ctx.enter_context(tc.psum_pool(name="psum_y", bufs=2))
         ctx.enter_context(tc.manual_schedule())
@@ -72,15 +71,20 @@ def tile_multiscaleretention_pa_kernel(
         x_codes = keep.tile([P, PASSES, 2 * T], U8, name="x_codes", align_bytes=64)
         x_plane = plane_tile(T, "x_plane")
         w_codes = {}
-        w_plane = {}
         for w in range(2):
             for ch in range(CHUNKS):
                 w_codes[w, ch] = keep.tile([P, PASSES, 2 * BANK], U8, name=f"w_codes_{w}_{ch}", align_bytes=64)
-            w_plane[w, 2] = plane_tile(BANK, f"w_plane_hi_{w}")
-            w_plane[w, 0] = plane_tile(2 * BANK, f"w_plane_lo_{w}")
+
+        q_high = plane_tile(BANK, "q_high")
+        q_low = plane_tile(2 * BANK, "q_low")
+        k_all = plane_tile(C, "k_all")
+        w_plane = {(0, 2): (q_high, 0), (1, 2): (k_all, 2 * BANK)}
+        for ch in range(2):
+            w_plane[0, ch] = (q_low, BANK * ch)
+            w_plane[1, ch] = (k_all, BANK * ch)
 
         zero(nc.vector, x_plane)
-        zero(nc.vector, w_plane[0, 2])
+        zero(nc.vector, q_high)
 
         arg = keep.tile([P, PAIRS], F32, name="arg")
         nc.gpsimd.iota(arg[:], pattern=[[10, PAIRS]], base=3072, channel_multiplier=0, allow_small_or_imprecise_dtypes=True)
@@ -88,16 +92,14 @@ def tile_multiscaleretention_pa_kernel(
         nc.gpsimd.iota(pos[:], pattern=[[P, TILES]], base=0, channel_multiplier=1, allow_small_or_imprecise_dtypes=True)
         pos_r = keep.tile([P, TILES], F32, name="pos_r")
         nc.gpsimd.tensor_scalar(out=pos_r[:], in0=pos[:], scalar1=1.0 / SCALE_BASE, scalar2=0.0, op0=ALU.mult, op1=ALU.add)
+        zero(nc.gpsimd, k_all)
         pos_a = keep.tile([P, TILES], F32, name="pos_a")
         nc.gpsimd.tensor_scalar(out=pos_a[:], in0=pos[:], scalar1=2.0 * math.pi, scalar2=0.0, op0=ALU.mult, op1=ALU.add)
         neg_a = keep.tile([P, TILES], F32, name="neg_a")
         nc.gpsimd.tensor_scalar(out=neg_a[:], in0=pos[:], scalar1=-2.0 * math.pi, scalar2=0.0, op0=ALU.mult, op1=ALU.add)
-
         half_pi = keep.tile([P, 1], F32, name="half_pi")
         nc.gpsimd.tensor_scalar(out=half_pi[:], in0=pos[:, 0:1], scalar1=0.0, scalar2=0.5 * math.pi, op0=ALU.mult, op1=ALU.add)
-        zero(nc.gpsimd, w_plane[1, 2])
-        zero(nc.gpsimd, w_plane[0, 0])
-        zero(nc.gpsimd, w_plane[1, 0])
+        zero(nc.gpsimd, q_low)
         ident = keep.tile([P, P], F32, name="ident")
         make_identity(nc, ident[:])
 
@@ -115,14 +117,14 @@ def tile_multiscaleretention_pa_kernel(
         load_codes(x_codes, x_words, 0, T)
         load_codes(w_codes[0, 2], words[0], 2 * BANK, BANK)
         load_scales(x_plane, x_scales, 0, T)
-        load_scales(w_plane[0, 2], scales[0], 2 * BANK, BANK)
+        load_scales(q_high, scales[0], 2 * BANK, BANK)
         load_codes(w_codes[1, 2], words[1], 2 * BANK, BANK)
-        load_scales(w_plane[1, 2], scales[1], 2 * BANK, BANK)
-        for w in range(2):
-            load_codes(w_codes[w, 1], words[w], BANK, BANK)
-            load_scales(w_plane[w, 0], scales[w], 0, 2 * BANK)
-        for w in range(2):
-            load_codes(w_codes[w, 0], words[w], 0, BANK)
+        load_scales(k_all, scales[1], 0, C)
+        load_codes(w_codes[0, 1], words[0], BANK, BANK)
+        load_scales(q_low, scales[0], 0, 2 * BANK)
+        load_codes(w_codes[1, 1], words[1], BANK, BANK)
+        load_codes(w_codes[0, 0], words[0], 0, BANK)
+        load_codes(w_codes[1, 0], words[1], 0, BANK)
 
         frac = {}
         decay = {}
@@ -131,13 +133,18 @@ def tile_multiscaleretention_pa_kernel(
         c_tab = {}
         s_tab = {}
 
+        turns = {}
+
+        def count_turns(i):
+            lim = DIRECT[i]
+            turns[i] = tabs.tile([P, LOW], I32, name="turns")
+            nc.vector.tensor_scalar(out=turns[i][:, :lim], in0=freq[:, :lim], scalar1=pos[:, i : i + 1], scalar2=None, op0=ALU.mult)
+
         def reduce_angle(i):
             lim = DIRECT[i]
-            turns = tabs.tile([P, LOW], I32, name="turns")
-            nc.vector.tensor_scalar(out=turns[:, :lim], in0=freq[:, :lim], scalar1=pos[:, i : i + 1], scalar2=None, op0=ALU.mult)
             f = tabs.tile([P, LOW], F32, name="frac")
             nc.vector.scalar_tensor_tensor(
-                out=f[:, :lim], in0=freq[:, :lim], scalar=pos[:, i : i + 1], in1=turns[:, :lim], op0=ALU.mult, op1=ALU.subtract
+                out=f[:, :lim], in0=freq[:, :lim], scalar=pos[:, i : i + 1], in1=turns[i][:, :lim], op0=ALU.mult, op1=ALU.subtract
             )
             frac[i] = f
 
@@ -167,24 +174,28 @@ def tile_multiscaleretention_pa_kernel(
 
         def make_s(engine, i, a=0, b=PAIRS):
             if i not in s_tab:
-                s_tab[i] = tabs.tile([P, PAIRS], F32, name="s_tab")
-            engine.tensor_tensor(out=s_tab[i][:, a:b], in0=sin[i][:, a:b], in1=decay[i][:, a:b], op=ALU.mult)
+                s_tab[i] = tabs.tile([P, 2, PAIRS], F32, name="s_tab")
+            engine.tensor_tensor(out=s_tab[i][:, 1, a:b], in0=sin[i][:, a:b], in1=decay[i][:, a:b], op=ALU.mult)
+
+        def negate_s(i):
+            nc.scalar.activation(out=s_tab[i][:, 0, :], in_=s_tab[i][:, 1, :], func=ACT.Copy, scale=-1.0)
 
         nc.scalar.activation(out=arg[:], in_=arg[:], func=ACT.Ln, scale=1.0 / 10752.0)
-        make_decay(0)
-        make_decay(1)
-        reduce_angle(0)
-        for i in range(1, TILES):
+        for i in range(TILES):
+            make_decay(i)
+        for i in range(TILES):
+            count_turns(i)
+        for i in range(TILES):
             reduce_angle(i)
         make_sin_cos(0, HEAD, PAIRS)
         make_sin_cos(0, 0, HEAD)
         make_sin_cos(1, 0, PAIRS)
+        make_sin_cos(2, 0, PAIRS)
 
         def project(i, w, ch):
             z = psum.tile([P, BANK], F32, name="z")
             tok = slice(P * i, P * (i + 1))
-            plane = w_plane[w, 2] if ch == 2 else w_plane[w, 0]
-            c0 = 0 if ch == 2 else BANK * ch
+            plane, c0 = w_plane[w, ch]
             for g in range(PASSES):
                 nc.tensor.matmul_mx(
                     out=z[:],
@@ -197,100 +208,120 @@ def tile_multiscaleretention_pa_kernel(
                 )
             return z
 
-        def times_cos(i, ch, z):
+        def times_cos(i, ch, z, a):
             j = slice(BANK_PAIRS * ch, BANK_PAIRS * (ch + 1))
-            a = work.tile([P, BANK], F32, name="a")
             nc.vector.tensor_tensor(
-                out=a[:].rearrange("p (t j) -> p t j", t=2),
-                in0=z[:].rearrange("p (j t) -> p t j", t=2),
-                in1=c_tab[i][:, j].unsqueeze(1).to_broadcast([P, 2, BANK_PAIRS]),
+                out=a.rearrange("p (t j) -> p t j", t=2),
+                in0=c_tab[i][:, j].unsqueeze(1).to_broadcast([P, 2, BANK_PAIRS]),
+                in1=z[:].rearrange("p (j t) -> p t j", t=2),
                 op=ALU.mult,
             )
-            return a
 
-        def times_sin(i, ch, z):
+        def times_sin(i, ch, z, b):
             j = slice(BANK_PAIRS * ch, BANK_PAIRS * (ch + 1))
-            z_pairs = z[:].rearrange("p (j t) -> p j t", t=2)
-            b = work.tile([P, BANK], F32, name="b")
-            nc.vector.scalar_tensor_tensor(
-                out=b[:, :BANK_PAIRS], in0=z_pairs[:, :, 1], scalar=-1.0, in1=s_tab[i][:, j], op0=ALU.mult, op1=ALU.mult
-            )
-            nc.vector.tensor_tensor(out=b[:, BANK_PAIRS:], in0=z_pairs[:, :, 0], in1=s_tab[i][:, j], op=ALU.mult)
-            return b
-
-        def store(n, y):
-            i, w, ch = banks[n]
-            nc.sync.dma_start(out=outs[w][0, P * i : P * (i + 1), BANK * ch : BANK * (ch + 1)], in_=y[:])
-
-        def add_on_vector(n, a, b):
-            y = work.tile([P, BANK], F32, name="y")
-            nc.vector.tensor_tensor(
-                out=y[:].rearrange("p (j t) -> p j t", t=2),
-                in0=a[:].rearrange("p (t j) -> p j t", t=2),
-                in1=b[:].rearrange("p (t j) -> p j t", t=2),
-                op=ALU.add,
-            )
-            store(n, y)
-
-        def interleave(n, d):
-            y = work.tile([P, BANK], F32, name="y")
-            nc.scalar.copy(
-                out=y[:].rearrange("p (j t) -> p j t", t=2), in_=d[:].rearrange("p (t j) -> p j t", t=2)
-            )
-            store(n, y)
-
-        def add_halves(n, a, b):
-            if ADDS[n] == "P":
-                d = psum_y.tile([P, BANK], F32, name="d_psum")
-                nc.tensor.matmul(out=d[:], lhsT=ident[:], rhs=a[:], start=True, stop=False)
-                nc.tensor.matmul(out=d[:], lhsT=ident[:], rhs=b[:], start=False, stop=True)
+            if i == 0:
+                z_pairs = z[:].rearrange("p (j t) -> p j t", t=2)
+                s = s_tab[i][:, 1, j]
+                nc.vector.scalar_tensor_tensor(
+                    out=b[:, :BANK_PAIRS], in0=s, scalar=-1.0, in1=z_pairs[:, :, 1], op0=ALU.mult, op1=ALU.mult
+                )
+                nc.vector.tensor_tensor(out=b[:, BANK_PAIRS:], in0=s, in1=z_pairs[:, :, 0], op=ALU.mult)
             else:
-                d = work.tile([P, BANK], F32, name="d")
+                nc.vector.tensor_tensor(
+                    out=b.rearrange("p (t j) -> p t j", t=2),
+                    in0=s_tab[i][:, :, j],
+                    in1=z[:].rearrange("p (j t) -> p t j", t=2)[:, ::-1, :],
+                    op=ALU.mult,
+                )
+
+        def store(m, w, y):
+            i, ch = pairs[m]
+            nc.sync.dma_start(out=outs[w][0, P * i : P * (i + 1), BANK * ch : BANK * (ch + 1)], in_=y)
+
+        def halves_to_pairs(d):
+            return d.rearrange("p (t j) -> p j t", t=2)
+
+        def pairs_view(y):
+            return y.rearrange("p (j t) -> p j t", t=2)
+
+        def add_on_vector(m, w, a, b):
+            y = work.tile([P, BANK], F32, name="y_one")
+            nc.vector.tensor_tensor(out=pairs_view(y[:]), in0=halves_to_pairs(a), in1=halves_to_pairs(b), op=ALU.add)
+            store(m, w, y[:])
+
+        def interleave(m, d):
+            y = work.tile([P, 2, BANK], F32, name="y")
+            if ADDS[m] == "P":
+                for w in range(2):
+                    nc.scalar.copy(out=pairs_view(y[:, w, :]), in_=halves_to_pairs(d[w][:]))
+            else:
+                nc.scalar.copy(
+                    out=y[:].rearrange("p w (j t) -> p w j t", t=2), in_=d[:].rearrange("p w (t j) -> p w j t", t=2)
+                )
+            for w in range(2):
+                store(m, w, y[:, w, :])
+
+        def add_halves(m, a, b):
+            if ADDS[m] == "P":
+                d = []
+                for w in range(2):
+                    total = psum_y.tile([P, BANK], F32, name="total")
+                    nc.tensor.matmul(out=total[:], lhsT=ident[:], rhs=a[:, w, :], start=True, stop=False)
+                    nc.tensor.matmul(out=total[:], lhsT=ident[:], rhs=b[:, w, :], start=False, stop=True)
+                    d.append(total)
+            else:
+                d = work.tile([P, 2, BANK], F32, name="d")
                 nc.gpsimd.tensor_tensor(out=d[:], in0=a[:], in1=b[:], op=ALU.add)
             return d
 
-        banks = [(i, w, ch) for i in range(TILES) for ch in (2, 1, 0) for w in range(2)]
+        pairs = [(i, ch) for i in range(TILES) for ch in (2, 1, 0)]
         z = {}
-        for n in range(LEAD):
-            z[n] = project(*banks[n])
+
+        def project_pair(m):
+            i, ch = pairs[m]
+            z[m] = [project(i, w, ch) for w in range(2)]
+
+        for m in range(LEAD):
+            project_pair(m)
         make_c(nc.vector, 0, HEAD, PAIRS)
-        halves = []
-        on_vector = []
-        for n, (i, w, ch) in enumerate(banks):
-            if n + LEAD < len(banks):
-                z[n + LEAD] = project(*banks[n + LEAD])
-            a = times_cos(i, ch, z[n])
-            if n == 0:
+        waiting = []
+        for m, (i, ch) in enumerate(pairs):
+            if m + LEAD < len(pairs):
+                project_pair(m + LEAD)
+            a = work.tile([P, 2, BANK], F32, name="a")
+            b = work.tile([P, 2, BANK], F32, name="b")
+            times_cos(i, ch, z[m][0], a[:, 0, :])
+            if m == 0:
                 make_s(nc.vector, 0, HEAD, PAIRS)
-            for args in on_vector:
-                add_on_vector(*args)
-            on_vector = []
-            b = times_sin(i, ch, z[n])
-            if ADDS[n] == "V":
-                on_vector.append((n, a, b))
+            if ADDS[m] == "V":
+                times_sin(i, ch, z[m][0], b[:, 0, :])
+                times_cos(i, ch, z[m][1], a[:, 1, :])
+                add_on_vector(m, 0, a[:, 0, :], b[:, 0, :])
+                times_sin(i, ch, z[m][1], b[:, 1, :])
+                add_on_vector(m, 1, a[:, 1, :], b[:, 1, :])
             else:
-                halves.append((n, add_halves(n, a, b)))
-            if n >= INTERLEAVE_FROM:
-                for args in halves:
-                    interleave(*args)
-                halves = []
-            if n == 0:
-                make_decay(2)
-            elif n == 1:
+                times_cos(i, ch, z[m][1], a[:, 1, :])
+                times_sin(i, ch, z[m][0], b[:, 0, :])
+                times_sin(i, ch, z[m][1], b[:, 1, :])
+                waiting.append((m, add_halves(m, a, b)))
+            while m >= 2 and waiting and waiting[0][0] <= m - 1:
+                interleave(*waiting.pop(0))
+            if m == 0:
                 make_c(nc.vector, 0, 0, HEAD)
                 make_s(nc.vector, 0, 0, HEAD)
                 make_c(nc.gpsimd, 1)
-                make_s(nc.vector, 1)
-                make_decay(3)
-            elif n == 4:
-                make_sin_cos(2, 0, PAIRS)
+                make_s(nc.gpsimd, 1)
+            elif m == 1:
+                negate_s(1)
                 make_s(nc.gpsimd, 2)
-                make_c(nc.gpsimd, 2)
-            elif n == 5:
+            elif m == 2:
+                negate_s(2)
+            elif m == 3:
                 make_sin_cos(3, 0, PAIRS)
-            elif n == 10:
+            elif m == 4:
                 make_s(nc.gpsimd, 3)
-            elif n == 12:
-                make_c(nc.gpsimd, 3)
-        for args in on_vector:
-            add_on_vector(*args)
+            elif m == 5:
+                make_c(nc.vector, 2)
+                make_c(nc.vector, 3)
+            elif m == 6:
+                negate_s(3)

@@ -29,7 +29,7 @@ DIRECT = (312, 368, 408, 432)
 LOW = DIRECT[-1]
 HEAD = 2 * BANK_PAIRS
 LEAD = 2
-ADDS = "GPGGPGGGGPGV"
+ADDS = "PGGGGGPGGPVL"
 
 
 def tile_multiscaleretention_pa_kernel(
@@ -43,7 +43,7 @@ def tile_multiscaleretention_pa_kernel(
     with ExitStack() as ctx:
         keep = ctx.enter_context(tc.tile_pool(name="keep", bufs=1))
         tabs = ctx.enter_context(tc.tile_pool(name="tabs", bufs=TILES))
-        work = ctx.enter_context(tc.tile_pool(name="work", bufs=5))
+        work = ctx.enter_context(tc.tile_pool(name="work", bufs=4))
         psum = ctx.enter_context(tc.psum_pool(name="psum", bufs=6))
         psum_y = ctx.enter_context(tc.psum_pool(name="psum_y", bufs=2))
         ctx.enter_context(tc.manual_schedule())
@@ -130,8 +130,7 @@ def tile_multiscaleretention_pa_kernel(
         decay = {}
         sin = {}
         cos = {}
-        c_tab = {}
-        s_tab = {}
+        table = {}
 
         turns = {}
 
@@ -167,18 +166,22 @@ def tile_multiscaleretention_pa_kernel(
             if a < lim:
                 nc.scalar.activation(out=sin[i][:, a:lim], in_=frac[i][:, a:lim], func=ACT.Sin, scale=2.0 * math.pi)
 
+        def make_row(engine, i, row, wave, a=0, b=PAIRS):
+            if i not in table:
+                table[i] = tabs.tile([P, 4, PAIRS], F32, name="table")
+            engine.tensor_tensor(out=table[i][:, row, a:b], in0=wave[i][:, a:b], in1=decay[i][:, a:b], op=ALU.mult)
+
         def make_c(engine, i, a=0, b=PAIRS):
-            if i not in c_tab:
-                c_tab[i] = tabs.tile([P, PAIRS], F32, name="c_tab")
-            engine.tensor_tensor(out=c_tab[i][:, a:b], in0=cos[i][:, a:b], in1=decay[i][:, a:b], op=ALU.mult)
+            make_row(engine, i, 0, cos, a, b)
 
         def make_s(engine, i, a=0, b=PAIRS):
-            if i not in s_tab:
-                s_tab[i] = tabs.tile([P, 2, PAIRS], F32, name="s_tab")
-            engine.tensor_tensor(out=s_tab[i][:, 1, a:b], in0=sin[i][:, a:b], in1=decay[i][:, a:b], op=ALU.mult)
+            make_row(engine, i, 2, sin, a, b)
+
+        def repeat_c(i):
+            nc.scalar.copy(out=table[i][:, 1, :], in_=table[i][:, 0, :])
 
         def negate_s(i):
-            nc.scalar.activation(out=s_tab[i][:, 0, :], in_=s_tab[i][:, 1, :], func=ACT.Copy, scale=-1.0)
+            nc.scalar.activation(out=table[i][:, 3, :], in_=table[i][:, 2, :], func=ACT.Copy, scale=-1.0)
 
         nc.scalar.activation(out=arg[:], in_=arg[:], func=ACT.Ln, scale=1.0 / 10752.0)
         for i in range(TILES):
@@ -208,70 +211,72 @@ def tile_multiscaleretention_pa_kernel(
                 )
             return z
 
-        def times_cos(i, ch, z, a):
-            j = slice(BANK_PAIRS * ch, BANK_PAIRS * (ch + 1))
+        def first_products(z, c, s, ab):
             nc.vector.tensor_tensor(
-                out=a.rearrange("p (t j) -> p t j", t=2),
-                in0=c_tab[i][:, j].unsqueeze(1).to_broadcast([P, 2, BANK_PAIRS]),
-                in1=z[:].rearrange("p (j t) -> p t j", t=2),
+                out=ab[:, 0:2, :], in0=c.unsqueeze(1).to_broadcast([P, 2, BANK_PAIRS]), in1=z[:].rearrange("p (j t) -> p t j", t=2), op=ALU.mult
+            )
+
+        def second_products(z, c, s, ab):
+            z_pairs = z[:].rearrange("p (j t) -> p j t", t=2)
+            nc.vector.tensor_tensor(out=ab[:, 2, :], in0=s, in1=z_pairs[:, :, 0], op=ALU.mult)
+            nc.vector.scalar_tensor_tensor(out=ab[:, 3, :], in0=s, scalar=-1.0, in1=z_pairs[:, :, 1], op0=ALU.mult, op1=ALU.mult)
+
+        def all_products(z, rows, ab):
+            nc.vector.tensor_tensor(
+                out=ab.rearrange("p (g t) j -> p g t j", t=2),
+                in0=rows.rearrange("p (g t) j -> p g t j", t=2),
+                in1=z[:].rearrange("p (j t) -> p t j", t=2).unsqueeze(1).to_broadcast([P, 2, 2, BANK_PAIRS]),
                 op=ALU.mult,
             )
 
-        def times_sin(i, ch, z, b):
-            j = slice(BANK_PAIRS * ch, BANK_PAIRS * (ch + 1))
-            if i == 0:
-                z_pairs = z[:].rearrange("p (j t) -> p j t", t=2)
-                s = s_tab[i][:, 1, j]
-                nc.vector.scalar_tensor_tensor(
-                    out=b[:, :BANK_PAIRS], in0=s, scalar=-1.0, in1=z_pairs[:, :, 1], op0=ALU.mult, op1=ALU.mult
-                )
-                nc.vector.tensor_tensor(out=b[:, BANK_PAIRS:], in0=s, in1=z_pairs[:, :, 0], op=ALU.mult)
-            else:
-                nc.vector.tensor_tensor(
-                    out=b.rearrange("p (t j) -> p t j", t=2),
-                    in0=s_tab[i][:, :, j],
-                    in1=z[:].rearrange("p (j t) -> p t j", t=2)[:, ::-1, :],
-                    op=ALU.mult,
-                )
-
-        def store(m, w, y):
+        def store(m, w, y, a=0, b=BANK):
             i, ch = pairs[m]
-            nc.sync.dma_start(out=outs[w][0, P * i : P * (i + 1), BANK * ch : BANK * (ch + 1)], in_=y)
+            nc.sync.dma_start(out=outs[w][0, P * i : P * (i + 1), BANK * ch + a : BANK * ch + b], in_=y)
 
-        def halves_to_pairs(d):
-            return d.rearrange("p (t j) -> p j t", t=2)
+        def add_on_vector(m, ab):
+            y = work.tile([P, 2, BANK], F32, name="y")
+            nc.vector.tensor_tensor(
+                out=y[:].rearrange("p w (j t) -> p w j t", t=2),
+                in0=ab[:, :, 0:2, :].rearrange("p w t j -> p w j t"),
+                in1=ab[:, :, 2:4, :][:, :, ::-1, :].rearrange("p w t j -> p w j t"),
+                op=ALU.add,
+            )
+            for w in range(2):
+                store(m, w, y[:, w, :])
 
-        def pairs_view(y):
-            return y.rearrange("p (j t) -> p j t", t=2)
-
-        def add_on_vector(m, w, a, b):
-            y = work.tile([P, BANK], F32, name="y_one")
-            nc.vector.tensor_tensor(out=pairs_view(y[:]), in0=halves_to_pairs(a), in1=halves_to_pairs(b), op=ALU.add)
-            store(m, w, y[:])
+        def add_part(m, w, ab, y, a, b):
+            j = slice(a // 2, b // 2)
+            nc.vector.tensor_tensor(
+                out=y[:, w, a:b].rearrange("p (j t) -> p j t", t=2),
+                in0=ab[:, w, 0:2, j].rearrange("p t j -> p j t"),
+                in1=ab[:, w, 2:4, j][:, ::-1, :].rearrange("p t j -> p j t"),
+                op=ALU.add,
+            )
+            store(m, w, y[:, w, a:b], a, b)
 
         def interleave(m, d):
             y = work.tile([P, 2, BANK], F32, name="y")
             if ADDS[m] == "P":
                 for w in range(2):
-                    nc.scalar.copy(out=pairs_view(y[:, w, :]), in_=halves_to_pairs(d[w][:]))
+                    nc.scalar.copy(out=y[:, w, :].rearrange("p (j t) -> p j t", t=2), in_=d[w][:].rearrange("p (t j) -> p j t", t=2))
             else:
-                nc.scalar.copy(
-                    out=y[:].rearrange("p w (j t) -> p w j t", t=2), in_=d[:].rearrange("p w (t j) -> p w j t", t=2)
-                )
+                nc.scalar.copy(out=y[:].rearrange("p w (j t) -> p w j t", t=2), in_=d[:].rearrange("p w t j -> p w j t"))
             for w in range(2):
                 store(m, w, y[:, w, :])
 
-        def add_halves(m, a, b):
+        def add_halves(m, ab):
             if ADDS[m] == "P":
                 d = []
                 for w in range(2):
                     total = psum_y.tile([P, BANK], F32, name="total")
-                    nc.tensor.matmul(out=total[:], lhsT=ident[:], rhs=a[:, w, :], start=True, stop=False)
-                    nc.tensor.matmul(out=total[:], lhsT=ident[:], rhs=b[:, w, :], start=False, stop=True)
+                    for t in range(2):
+                        half = total[:, BANK_PAIRS * t : BANK_PAIRS * (t + 1)]
+                        nc.tensor.matmul(out=half, lhsT=ident[:], rhs=ab[:, w, t, :], start=True, stop=False)
+                        nc.tensor.matmul(out=half, lhsT=ident[:], rhs=ab[:, w, 3 - t, :], start=False, stop=True)
                     d.append(total)
             else:
-                d = work.tile([P, 2, BANK], F32, name="d")
-                nc.gpsimd.tensor_tensor(out=d[:], in0=a[:], in1=b[:], op=ALU.add)
+                d = work.tile([P, 2, 2, BANK_PAIRS], F32, name="d")
+                nc.gpsimd.tensor_tensor(out=d[:], in0=ab[:, :, 0:2, :], in1=ab[:, :, 2:4, :][:, :, ::-1, :], op=ALU.add)
             return d
 
         pairs = [(i, ch) for i in range(TILES) for ch in (2, 1, 0)]
@@ -288,40 +293,47 @@ def tile_multiscaleretention_pa_kernel(
         for m, (i, ch) in enumerate(pairs):
             if m + LEAD < len(pairs):
                 project_pair(m + LEAD)
-            a = work.tile([P, 2, BANK], F32, name="a")
-            b = work.tile([P, 2, BANK], F32, name="b")
-            times_cos(i, ch, z[m][0], a[:, 0, :])
-            if m == 0:
-                make_s(nc.vector, 0, HEAD, PAIRS)
-            if ADDS[m] == "V":
-                times_sin(i, ch, z[m][0], b[:, 0, :])
-                times_cos(i, ch, z[m][1], a[:, 1, :])
-                add_on_vector(m, 0, a[:, 0, :], b[:, 0, :])
-                times_sin(i, ch, z[m][1], b[:, 1, :])
-                add_on_vector(m, 1, a[:, 1, :], b[:, 1, :])
+            j = slice(BANK_PAIRS * ch, BANK_PAIRS * (ch + 1))
+            ab = work.tile([P, 2, 4, BANK_PAIRS], F32, name="ab")
+            if i == 0:
+                if m == 0:
+                    make_s(nc.gpsimd, 0, HEAD, PAIRS)
+                c, s = table[i][:, 0, j], table[i][:, 2, j]
+                for w in range(2):
+                    first_products(z[m][w], c, s, ab[:, w, :, :])
+                for w in range(2):
+                    second_products(z[m][w], c, s, ab[:, w, :, :])
             else:
-                times_cos(i, ch, z[m][1], a[:, 1, :])
-                times_sin(i, ch, z[m][0], b[:, 0, :])
-                times_sin(i, ch, z[m][1], b[:, 1, :])
-                waiting.append((m, add_halves(m, a, b)))
-            while m >= 2 and waiting and waiting[0][0] <= m - 1:
+                for w in range(2):
+                    all_products(z[m][w], table[i][:, :, j], ab[:, w, :, :])
+            if ADDS[m] == "V":
+                add_on_vector(m, ab)
+            elif ADDS[m] == "L":
+                y = work.tile([P, 2, BANK], F32, name="y")
+                add_part(m, 0, ab, y, 0, BANK)
+                add_part(m, 1, ab, y, 0, BANK_PAIRS)
+                add_part(m, 1, ab, y, BANK_PAIRS, BANK)
+            else:
+                waiting.append((m, add_halves(m, ab)))
+            while m >= 4 and waiting and waiting[0][0] <= m - 1:
                 interleave(*waiting.pop(0))
             if m == 0:
-                make_c(nc.vector, 0, 0, HEAD)
-                make_s(nc.vector, 0, 0, HEAD)
+                make_c(nc.gpsimd, 0, 0, HEAD)
+                make_s(nc.gpsimd, 0, 0, HEAD)
                 make_c(nc.gpsimd, 1)
-                make_s(nc.gpsimd, 1)
+                repeat_c(1)
             elif m == 1:
-                negate_s(1)
-                make_s(nc.gpsimd, 2)
+                make_s(nc.vector, 1)
+                make_c(nc.vector, 2)
             elif m == 2:
-                negate_s(2)
+                make_s(nc.gpsimd, 2)
+                repeat_c(2)
+                negate_s(1)
             elif m == 3:
                 make_sin_cos(3, 0, PAIRS)
+                negate_s(2)
             elif m == 4:
+                make_c(nc.gpsimd, 3)
                 make_s(nc.gpsimd, 3)
-            elif m == 5:
-                make_c(nc.vector, 2)
-                make_c(nc.vector, 3)
-            elif m == 6:
+                repeat_c(3)
                 negate_s(3)

@@ -29,7 +29,7 @@ DIRECT = (312, 368, 408, 432)
 LOW = DIRECT[-1]
 HEAD = 2 * BANK_PAIRS
 LEAD = 2
-ADDS = "PGGGGGPGGPVL"
+ADDS = "PGGGGPGGGPVL"
 
 
 def tile_multiscaleretention_pa_kernel(
@@ -44,6 +44,7 @@ def tile_multiscaleretention_pa_kernel(
         keep = ctx.enter_context(tc.tile_pool(name="keep", bufs=1))
         tabs = ctx.enter_context(tc.tile_pool(name="tabs", bufs=TILES))
         work = ctx.enter_context(tc.tile_pool(name="work", bufs=4))
+        prods = ctx.enter_context(tc.tile_pool(name="prods", bufs=6))
         psum = ctx.enter_context(tc.psum_pool(name="psum", bufs=6))
         psum_y = ctx.enter_context(tc.psum_pool(name="psum_y", bufs=2))
         ctx.enter_context(tc.manual_schedule())
@@ -147,6 +148,18 @@ def tile_multiscaleretention_pa_kernel(
             )
             frac[i] = f
 
+        mag = {}
+
+        def fold_angle(engine, i):
+            lim = DIRECT[i]
+            mag[i] = tabs.tile([P, LOW], F32, name="mag")
+            if engine is nc.vector:
+                nc.vector.scalar_tensor_tensor(
+                    out=mag[i][:, :lim], in0=frac[i][:, :lim], scalar=-1.0, in1=frac[i][:, :lim], op0=ALU.mult, op1=ALU.max
+                )
+            else:
+                nc.scalar.activation(out=mag[i][:, :lim], in_=frac[i][:, :lim], func=ACT.Abs)
+
         def make_decay(i):
             decay[i] = tabs.tile([P, PAIRS], F32, name="decay")
             nc.scalar.activation(out=decay[i][:], in_=arg[:], func=ACT.Exp, scale=pos_r[:, i : i + 1])
@@ -159,9 +172,9 @@ def tile_multiscaleretention_pa_kernel(
             lo = max(a, lim)
             nc.scalar.activation(out=cos[i][:, lo:b], in_=freq[:, lo:b], func=ACT.Sin, scale=neg_a[:, i : i + 1], bias=half_pi[:, 0:1])
             if a < lim:
-                mag = tabs.tile([P, LOW], F32, name="mag")
-                nc.scalar.activation(out=mag[:, a:lim], in_=frac[i][:, a:lim], func=ACT.Abs)
-                nc.scalar.activation(out=cos[i][:, a:lim], in_=mag[:, a:lim], func=ACT.Sin, scale=-2.0 * math.pi, bias=half_pi[:, 0:1])
+                if i not in mag:
+                    fold_angle(nc.scalar, i)
+                nc.scalar.activation(out=cos[i][:, a:lim], in_=mag[i][:, a:lim], func=ACT.Sin, scale=-2.0 * math.pi, bias=half_pi[:, 0:1])
             nc.scalar.activation(out=sin[i][:, lo:b], in_=freq[:, lo:b], func=ACT.Sin, scale=pos_a[:, i : i + 1])
             if a < lim:
                 nc.scalar.activation(out=sin[i][:, a:lim], in_=frac[i][:, a:lim], func=ACT.Sin, scale=2.0 * math.pi)
@@ -184,16 +197,18 @@ def tile_multiscaleretention_pa_kernel(
             nc.scalar.activation(out=table[i][:, 3, :], in_=table[i][:, 2, :], func=ACT.Copy, scale=-1.0)
 
         nc.scalar.activation(out=arg[:], in_=arg[:], func=ACT.Ln, scale=1.0 / 10752.0)
-        for i in range(TILES):
+        for i in range(3):
             make_decay(i)
         for i in range(TILES):
             count_turns(i)
         for i in range(TILES):
             reduce_angle(i)
+        fold_angle(nc.vector, 0)
+        fold_angle(nc.vector, 1)
+        fold_angle(nc.vector, 2)
         make_sin_cos(0, HEAD, PAIRS)
         make_sin_cos(0, 0, HEAD)
         make_sin_cos(1, 0, PAIRS)
-        make_sin_cos(2, 0, PAIRS)
 
         def project(i, w, ch):
             z = psum.tile([P, BANK], F32, name="z")
@@ -259,10 +274,15 @@ def tile_multiscaleretention_pa_kernel(
             if ADDS[m] == "P":
                 for w in range(2):
                     nc.scalar.copy(out=y[:, w, :].rearrange("p (j t) -> p j t", t=2), in_=d[w][:].rearrange("p (t j) -> p j t", t=2))
+                    store(m, w, y[:, w, :])
+            elif ADDS[m] == "g":
+                for w in range(2):
+                    nc.scalar.copy(out=y[:, w, :].rearrange("p (j t) -> p j t", t=2), in_=d[:, w, :, :].rearrange("p t j -> p j t"))
+                    store(m, w, y[:, w, :])
             else:
                 nc.scalar.copy(out=y[:].rearrange("p w (j t) -> p w j t", t=2), in_=d[:].rearrange("p w t j -> p w j t"))
-            for w in range(2):
-                store(m, w, y[:, w, :])
+                for w in range(2):
+                    store(m, w, y[:, w, :])
 
         def add_halves(m, ab):
             if ADDS[m] == "P":
@@ -276,6 +296,10 @@ def tile_multiscaleretention_pa_kernel(
                     d.append(total)
             else:
                 d = work.tile([P, 2, 2, BANK_PAIRS], F32, name="d")
+                if ADDS[m] == "g":
+                    for w in range(2):
+                        nc.gpsimd.tensor_tensor(out=d[:, w], in0=ab[:, w, 0:2, :], in1=ab[:, w, 2:4, :][:, ::-1, :], op=ALU.add)
+                    return d
                 nc.gpsimd.tensor_tensor(out=d[:], in0=ab[:, :, 0:2, :], in1=ab[:, :, 2:4, :][:, :, ::-1, :], op=ALU.add)
             return d
 
@@ -294,7 +318,7 @@ def tile_multiscaleretention_pa_kernel(
             if m + LEAD < len(pairs):
                 project_pair(m + LEAD)
             j = slice(BANK_PAIRS * ch, BANK_PAIRS * (ch + 1))
-            ab = work.tile([P, 2, 4, BANK_PAIRS], F32, name="ab")
+            ab = prods.tile([P, 2, 4, BANK_PAIRS], F32, name="ab")
             if i == 0:
                 if m == 0:
                     make_s(nc.gpsimd, 0, HEAD, PAIRS)
@@ -315,25 +339,28 @@ def tile_multiscaleretention_pa_kernel(
                 add_part(m, 1, ab, y, BANK_PAIRS, BANK)
             else:
                 waiting.append((m, add_halves(m, ab)))
-            while m >= 4 and waiting and waiting[0][0] <= m - 1:
+            while m >= 3 and waiting and waiting[0][0] <= m - 1:
                 interleave(*waiting.pop(0))
             if m == 0:
                 make_c(nc.gpsimd, 0, 0, HEAD)
-                make_s(nc.gpsimd, 0, 0, HEAD)
-                make_c(nc.gpsimd, 1)
+                make_s(nc.vector, 0, 0, HEAD)
+                make_c(nc.vector, 1)
+                make_s(nc.gpsimd, 1)
+                make_sin_cos(2, 0, PAIRS)
+                make_c(nc.gpsimd, 2)
                 repeat_c(1)
             elif m == 1:
-                make_s(nc.vector, 1)
-                make_c(nc.vector, 2)
-            elif m == 2:
-                make_s(nc.gpsimd, 2)
-                repeat_c(2)
                 negate_s(1)
-            elif m == 3:
+            elif m == 2:
                 make_sin_cos(3, 0, PAIRS)
+                make_decay(3)
+            elif m == 3:
+                make_s(nc.vector, 2)
+                repeat_c(2)
                 negate_s(2)
             elif m == 4:
                 make_c(nc.gpsimd, 3)
+            elif m == 5:
                 make_s(nc.gpsimd, 3)
                 repeat_c(3)
                 negate_s(3)

import math
from contextlib import ExitStack

import concourse.mybir as mybir
from concourse.masks import make_identity

F32 = mybir.dt.float32
I32 = mybir.dt.int32
U8 = mybir.dt.uint8
FP4X4 = mybir.dt.float4_e2m1fn_x4
ALU = mybir.AluOpType
ACT = mybir.ActivationFunctionType

P = 128
T = 512
E = 1536
C = 1536
PASSES = E // 512
TILES = T // P
PAIRS = C // 2
BANK = 512
BANK_PAIRS = BANK // 2
CHUNKS = C // BANK
SCALE_BASE = 512.0

FLOPS = 2 * 2 * T * E * C

DIRECT = (312, 368, 408, 432)
LOW = DIRECT[-1]
HEAD = 2 * BANK_PAIRS
LEAD = 2
ADDS = "PGGGGPGGGPVL"


def tile_multiscaleretention_pa_kernel(
    tc, x_words, x_scales, w_q_words, w_q_scales, w_k_words, w_k_scales, out_0, out_1
):
    nc = tc.nc
    words = (w_q_words, w_k_words)
    scales = (w_q_scales, w_k_scales)
    outs = (out_0, out_1)

    with ExitStack() as ctx:
        keep = ctx.enter_context(tc.tile_pool(name="keep", bufs=1))
        tabs = ctx.enter_context(tc.tile_pool(name="tabs", bufs=TILES))
        work = ctx.enter_context(tc.tile_pool(name="work", bufs=4))
        prods = ctx.enter_context(tc.tile_pool(name="prods", bufs=6))
        psum = ctx.enter_context(tc.psum_pool(name="psum", bufs=6))
        psum_y = ctx.enter_context(tc.psum_pool(name="psum_y", bufs=2))
        ctx.enter_context(tc.manual_schedule())

        def plane_tile(cols, name):
            t = keep.tile([P, PASSES, cols], U8, name=name, align_bytes=64)
            return t

        def zero(engine, plane):
            engine.memset(plane[:].rearrange("p g n -> p (g n)").bitcast(I32), 0)

        def load_codes(tile, src, c0, cols):
            nc.sync.dma_start(
                out=tile[:].bitcast(I32),
                in_=src[:, :, 2 * c0 : 2 * (c0 + cols)].rearrange("g p b -> p g b").bitcast(I32),
            )

        def load_scales(plane, src, c0, cols):
            for quad in range(4):
                nc.sync.dma_start(
                    out=plane[32 * quad : 32 * quad + 4, :, :].bitcast(I32),
                    in_=src[:, 4 * quad : 4 * quad + 4, c0 : c0 + cols].rearrange("g r n -> r g n").bitcast(I32),
                )

        x_codes = keep.tile([P, PASSES, 2 * T], U8, name="x_codes", align_bytes=64)
        x_plane = plane_tile(T, "x_plane")
        w_codes = {}
        for w in range(2):
            for ch in range(CHUNKS):
                w_codes[w, ch] = keep.tile([P, PASSES, 2 * BANK], U8, name=f"w_codes_{w}_{ch}", align_bytes=64)

        q_high = plane_tile(BANK, "q_high")
        q_low = plane_tile(2 * BANK, "q_low")
        k_all = plane_tile(C, "k_all")
        w_plane = {(0, 2): (q_high, 0), (1, 2): (k_all, 2 * BANK)}
        for ch in range(2):
            w_plane[0, ch] = (q_low, BANK * ch)
            w_plane[1, ch] = (k_all, BANK * ch)

        zero(nc.vector, x_plane)
        zero(nc.vector, q_high)

        arg = keep.tile([P, PAIRS], F32, name="arg")
        nc.gpsimd.iota(arg[:], pattern=[[10, PAIRS]], base=3072, channel_multiplier=0, allow_small_or_imprecise_dtypes=True)
        pos = keep.tile([P, TILES], F32, name="pos")
        nc.gpsimd.iota(pos[:], pattern=[[P, TILES]], base=0, channel_multiplier=1, allow_small_or_imprecise_dtypes=True)
        pos_r = keep.tile([P, TILES], F32, name="pos_r")
        nc.gpsimd.tensor_scalar(out=pos_r[:], in0=pos[:], scalar1=1.0 / SCALE_BASE, scalar2=0.0, op0=ALU.mult, op1=ALU.add)
        zero(nc.gpsimd, k_all)
        pos_a = keep.tile([P, TILES], F32, name="pos_a")
        nc.gpsimd.tensor_scalar(out=pos_a[:], in0=pos[:], scalar1=2.0 * math.pi, scalar2=0.0, op0=ALU.mult, op1=ALU.add)
        neg_a = keep.tile([P, TILES], F32, name="neg_a")
        nc.gpsimd.tensor_scalar(out=neg_a[:], in0=pos[:], scalar1=-2.0 * math.pi, scalar2=0.0, op0=ALU.mult, op1=ALU.add)
        half_pi = keep.tile([P, 1], F32, name="half_pi")
        nc.gpsimd.tensor_scalar(out=half_pi[:], in0=pos[:, 0:1], scalar1=0.0, scalar2=0.5 * math.pi, op0=ALU.mult, op1=ALU.add)
        zero(nc.gpsimd, q_low)
        ident = keep.tile([P, P], F32, name="ident")
        make_identity(nc, ident[:])

        freq = keep.tile([P, PAIRS], F32, name="freq")
        nc.vector.memset(freq[:, 0:1], 1.0)
        nc.vector.tensor_scalar(out=freq[:, 0:1], in0=freq[:, 0:1], scalar1=0.5 / math.pi, scalar2=None, op0=ALU.mult)
        have = 1
        while have < PAIRS:
            n = min(have, PAIRS - have)
            nc.vector.tensor_scalar(
                out=freq[:, have : have + n], in0=freq[:, 0:n], scalar1=10000.0 ** (-have / PAIRS), scalar2=None, op0=ALU.mult
            )
            have += n

        load_codes(x_codes, x_words, 0, T)
        load_codes(w_codes[0, 2], words[0], 2 * BANK, BANK)
        load_scales(x_plane, x_scales, 0, T)
        load_scales(q_high, scales[0], 2 * BANK, BANK)
        load_codes(w_codes[1, 2], words[1], 2 * BANK, BANK)
        load_scales(k_all, scales[1], 0, C)
        load_codes(w_codes[0, 1], words[0], BANK, BANK)
        load_scales(q_low, scales[0], 0, 2 * BANK)
        load_codes(w_codes[1, 1], words[1], BANK, BANK)
        load_codes(w_codes[0, 0], words[0], 0, BANK)
        load_codes(w_codes[1, 0], words[1], 0, BANK)

        frac = {}
        decay = {}
        sin = {}
        cos = {}
        table = {}

        turns = {}

        def count_turns(i):
            lim = DIRECT[i]
            turns[i] = tabs.tile([P, LOW], I32, name="turns")
            nc.vector.tensor_scalar(out=turns[i][:, :lim], in0=freq[:, :lim], scalar1=pos[:, i : i + 1], scalar2=None, op0=ALU.mult)

        def reduce_angle(i):
            lim = DIRECT[i]
            f = tabs.tile([P, LOW], F32, name="frac")
            nc.vector.scalar_tensor_tensor(
                out=f[:, :lim], in0=freq[:, :lim], scalar=pos[:, i : i + 1], in1=turns[i][:, :lim], op0=ALU.mult, op1=ALU.subtract
            )
            frac[i] = f

        mag = {}

        def fold_angle(engine, i):
            lim = DIRECT[i]
            mag[i] = tabs.tile([P, LOW], F32, name="mag")
            if engine is nc.vector:
                nc.vector.scalar_tensor_tensor(
                    out=mag[i][:, :lim], in0=frac[i][:, :lim], scalar=-1.0, in1=frac[i][:, :lim], op0=ALU.mult, op1=ALU.max
                )
            else:
                nc.scalar.activation(out=mag[i][:, :lim], in_=frac[i][:, :lim], func=ACT.Abs)

        def make_decay(i):
            decay[i] = tabs.tile([P, PAIRS], F32, name="decay")
            nc.scalar.activation(out=decay[i][:], in_=arg[:], func=ACT.Exp, scale=pos_r[:, i : i + 1])

        def make_sin_cos(i, a, b):
            lim = DIRECT[i]
            if i not in sin:
                sin[i] = tabs.tile([P, PAIRS], F32, name="sin")
                cos[i] = tabs.tile([P, PAIRS], F32, name="cos")
            lo = max(a, lim)
            nc.scalar.activation(out=cos[i][:, lo:b], in_=freq[:, lo:b], func=ACT.Sin, scale=neg_a[:, i : i + 1], bias=half_pi[:, 0:1])
            if a < lim:
                if i not in mag:
                    fold_angle(nc.scalar, i)
                nc.scalar.activation(out=cos[i][:, a:lim], in_=mag[i][:, a:lim], func=ACT.Sin, scale=-2.0 * math.pi, bias=half_pi[:, 0:1])
            nc.scalar.activation(out=sin[i][:, lo:b], in_=freq[:, lo:b], func=ACT.Sin, scale=pos_a[:, i : i + 1])
            if a < lim:
                nc.scalar.activation(out=sin[i][:, a:lim], in_=frac[i][:, a:lim], func=ACT.Sin, scale=2.0 * math.pi)

        def make_row(engine, i, row, wave, a=0, b=PAIRS):
            if i not in table:
                table[i] = tabs.tile([P, 4, PAIRS], F32, name="table")
            engine.tensor_tensor(out=table[i][:, row, a:b], in0=wave[i][:, a:b], in1=decay[i][:, a:b], op=ALU.mult)

        def make_c(engine, i, a=0, b=PAIRS):
            make_row(engine, i, 0, cos, a, b)

        def make_s(engine, i, a=0, b=PAIRS):
            make_row(engine, i, 2, sin, a, b)

        def repeat_c(i):
            nc.scalar.copy(out=table[i][:, 1, :], in_=table[i][:, 0, :])

        def negate_s(i):
            nc.scalar.activation(out=table[i][:, 3, :], in_=table[i][:, 2, :], func=ACT.Copy, scale=-1.0)

        nc.scalar.activation(out=arg[:], in_=arg[:], func=ACT.Ln, scale=1.0 / 10752.0)
        for i in range(3):
            make_decay(i)
        for i in range(TILES):
            count_turns(i)
        for i in range(TILES):
            reduce_angle(i)
        fold_angle(nc.vector, 0)
        fold_angle(nc.vector, 1)
        fold_angle(nc.vector, 2)
        make_sin_cos(0, HEAD, PAIRS)
        make_sin_cos(0, 0, HEAD)
        make_sin_cos(1, 0, PAIRS)

        def project(i, w, ch):
            z = psum.tile([P, BANK], F32, name="z")
            tok = slice(P * i, P * (i + 1))
            plane, c0 = w_plane[w, ch]
            for g in range(PASSES):
                nc.tensor.matmul_mx(
                    out=z[:],
                    lhsT=x_codes[:, g, 2 * P * i : 2 * P * (i + 1)].bitcast(FP4X4),
                    lhsT_scale=x_plane[:, g, tok],
                    rhs=w_codes[w, ch][:, g, :].bitcast(FP4X4),
                    rhs_scale=plane[:, g, c0 : c0 + BANK],
                    start=(g == 0),
                    stop=(g == PASSES - 1),
                )
            return z

        def first_products(z, c, s, ab):
            nc.vector.tensor_tensor(
                out=ab[:, 0:2, :], in0=c.unsqueeze(1).to_broadcast([P, 2, BANK_PAIRS]), in1=z[:].rearrange("p (j t) -> p t j", t=2), op=ALU.mult
            )

        def second_products(z, c, s, ab):
            z_pairs = z[:].rearrange("p (j t) -> p j t", t=2)
            nc.vector.tensor_tensor(out=ab[:, 2, :], in0=s, in1=z_pairs[:, :, 0], op=ALU.mult)
            nc.vector.scalar_tensor_tensor(out=ab[:, 3, :], in0=s, scalar=-1.0, in1=z_pairs[:, :, 1], op0=ALU.mult, op1=ALU.mult)

        def all_products(z, rows, ab):
            nc.vector.tensor_tensor(
                out=ab.rearrange("p (g t) j -> p g t j", t=2),
                in0=rows.rearrange("p (g t) j -> p g t j", t=2),
                in1=z[:].rearrange("p (j t) -> p t j", t=2).unsqueeze(1).to_broadcast([P, 2, 2, BANK_PAIRS]),
                op=ALU.mult,
            )

        def store(m, w, y, a=0, b=BANK):
            i, ch = pairs[m]
            nc.sync.dma_start(out=outs[w][0, P * i : P * (i + 1), BANK * ch + a : BANK * ch + b], in_=y)

        def add_on_vector(m, ab):
            y = work.tile([P, 2, BANK], F32, name="y")
            nc.vector.tensor_tensor(
                out=y[:].rearrange("p w (j t) -> p w j t", t=2),
                in0=ab[:, :, 0:2, :].rearrange("p w t j -> p w j t"),
                in1=ab[:, :, 2:4, :][:, :, ::-1, :].rearrange("p w t j -> p w j t"),
                op=ALU.add,
            )
            for w in range(2):
                store(m, w, y[:, w, :])

        def add_part(m, w, ab, y, a, b):
            j = slice(a // 2, b // 2)
            nc.vector.tensor_tensor(
                out=y[:, w, a:b].rearrange("p (j t) -> p j t", t=2),
                in0=ab[:, w, 0:2, j].rearrange("p t j -> p j t"),
                in1=ab[:, w, 2:4, j][:, ::-1, :].rearrange("p t j -> p j t"),
                op=ALU.add,
            )
            store(m, w, y[:, w, a:b], a, b)

        def interleave(m, d):
            y = work.tile([P, 2, BANK], F32, name="y")
            if ADDS[m] == "P":
                for w in range(2):
                    nc.scalar.copy(out=y[:, w, :].rearrange("p (j t) -> p j t", t=2), in_=d[w][:].rearrange("p (t j) -> p j t", t=2))
                    store(m, w, y[:, w, :])
            elif ADDS[m] == "g":
                for w in range(2):
                    nc.scalar.copy(out=y[:, w, :].rearrange("p (j t) -> p j t", t=2), in_=d[:, w, :, :].rearrange("p t j -> p j t"))
                    store(m, w, y[:, w, :])
            else:
                nc.scalar.copy(out=y[:].rearrange("p w (j t) -> p w j t", t=2), in_=d[:].rearrange("p w t j -> p w j t"))
                for w in range(2):
                    store(m, w, y[:, w, :])

        def add_halves(m, ab):
            if ADDS[m] == "P":
                d = []
                for w in range(2):
                    total = psum_y.tile([P, BANK], F32, name="total")
                    for t in range(2):
                        half = total[:, BANK_PAIRS * t : BANK_PAIRS * (t + 1)]
                        nc.tensor.matmul(out=half, lhsT=ident[:], rhs=ab[:, w, t, :], start=True, stop=False)
                        nc.tensor.matmul(out=half, lhsT=ident[:], rhs=ab[:, w, 3 - t, :], start=False, stop=True)
                    d.append(total)
            else:
                d = work.tile([P, 2, 2, BANK_PAIRS], F32, name="d")
                if ADDS[m] == "g":
                    for w in range(2):
                        nc.gpsimd.tensor_tensor(out=d[:, w], in0=ab[:, w, 0:2, :], in1=ab[:, w, 2:4, :][:, ::-1, :], op=ALU.add)
                    return d
                nc.gpsimd.tensor_tensor(out=d[:], in0=ab[:, :, 0:2, :], in1=ab[:, :, 2:4, :][:, :, ::-1, :], op=ALU.add)
            return d

        pairs = [(i, ch) for i in range(TILES) for ch in (2, 1, 0)]
        z = {}

        def project_pair(m):
            i, ch = pairs[m]
            z[m] = [project(i, w, ch) for w in range(2)]

        for m in range(LEAD):
            project_pair(m)
        make_c(nc.vector, 0, HEAD, PAIRS)
        waiting = []
        for m, (i, ch) in enumerate(pairs):
            if m + LEAD < len(pairs):
                project_pair(m + LEAD)
            j = slice(BANK_PAIRS * ch, BANK_PAIRS * (ch + 1))
            ab = prods.tile([P, 2, 4, BANK_PAIRS], F32, name="ab")
            if i == 0:
                if m == 0:
                    make_s(nc.gpsimd, 0, HEAD, PAIRS)
                c, s = table[i][:, 0, j], table[i][:, 2, j]
                for w in range(2):
                    first_products(z[m][w], c, s, ab[:, w, :, :])
                for w in range(2):
                    second_products(z[m][w], c, s, ab[:, w, :, :])
            else:
                for w in range(2):
                    all_products(z[m][w], table[i][:, :, j], ab[:, w, :, :])
            if ADDS[m] == "V":
                add_on_vector(m, ab)
            elif ADDS[m] == "L":
                y = work.tile([P, 2, BANK], F32, name="y")
                add_part(m, 0, ab, y, 0, BANK)
                add_part(m, 1, ab, y, 0, BANK_PAIRS)
                add_part(m, 1, ab, y, BANK_PAIRS, BANK)
            else:
                waiting.append((m, add_halves(m, ab)))
            while m >= 3 and waiting and waiting[0][0] <= m - 1:
                interleave(*waiting.pop(0))
            if m == 0:
                make_c(nc.gpsimd, 0, 0, HEAD)
                make_s(nc.vector, 0, 0, HEAD)
                make_c(nc.vector, 1)
                make_s(nc.gpsimd, 1)
                make_sin_cos(2, 0, PAIRS)
                make_c(nc.gpsimd, 2)
                repeat_c(1)
            elif m == 1:
                negate_s(1)
            elif m == 2:
                make_sin_cos(3, 0, PAIRS)
                make_decay(3)
            elif m == 3:
                make_s(nc.vector, 2)
                repeat_c(2)
                negate_s(2)
            elif m == 4:
                make_c(nc.gpsimd, 3)
            elif m == 5:
                make_s(nc.gpsimd, 3)
                repeat_c(3)
                negate_s(3)
